import numpy as np
import ml_dtypes


def mxq(x, axis, fmt="e4m3"):
    dtype, down = {"e4m3": (ml_dtypes.float8_e4m3fn, 7), "e5m2": (ml_dtypes.float8_e5m2, 14)}[fmt]
    v = np.moveaxis(np.asarray(x, np.float32).astype(ml_dtypes.bfloat16).astype(np.float64), axis, -1)
    blocks = v.reshape(v.shape[:-1] + (-1, 32))
    amax = np.abs(blocks).max(-1, keepdims=True)
    byte = np.maximum(np.where(amax > 0, np.frexp(amax)[1] - 1 + 127, 0) - down, 1)
    scale = np.exp2(byte - 127.0)
    codes = (blocks / scale).astype(np.float32).astype(dtype).astype(np.float64)
    return np.moveaxis((codes * scale).reshape(v.shape), -1, axis)


WIDE = False


def mx_kscale(k):
    if not WIDE:
        return np.ones(k)
    levels = np.array([10, -10, 5, -5, 0])
    a = np.random.permutation(np.resize(levels, k // 512 * 4)).reshape(k // 512, 4)
    idx = np.arange(k)
    return np.exp2(a[idx // 512, idx % 128 // 32])


BF16 = ml_dtypes.bfloat16


def bf(x):
    return np.asarray(x, np.float32).astype(BF16)


def f64(x):
    return np.asarray(x).astype(np.float64)


N, C, E, T, H, CK = 3, 512, 512, 1024, 8, 64
EPS = 1e-5


def setup_inputs():
    s = mx_kscale(C)
    return {
        "h_attn": bf(np.random.standard_normal((N, T, C)) * 0.4 * s),
        "x": bf(np.random.standard_normal((N, E, T))),
        "masks": bf(np.random.uniform(0.2, 1.0, (N, 1, T))),
        "Wo": bf(np.random.standard_normal((E, C)) * 2.0 / np.sqrt(C) / s[None, :]),
        "bo": bf(np.random.standard_normal(E) * 0.5),
    }


def reference(h_attn, x, masks, Wo, bo):
    o = (mxq(f64(h_attn), 2, "e4m3") @ mxq(f64(Wo), 1, "e4m3").T) + f64(bo)
    y = o.transpose(0, 2, 1) * f64(masks) + f64(x)
    mean = y.mean(-1, keepdims=True)
    var = np.square(y - mean).mean(-1, keepdims=True)
    return (y - mean) / np.sqrt(var + EPS)

@@ -1,0 +1,213 @@
+from contextlib import ExitStack
+
+import concourse.mybir as mybir
+from concourse.masks import make_identity
+
+F32 = mybir.dt.float32
+BF16 = mybir.dt.bfloat16
+U32 = mybir.dt.uint32
+U8 = mybir.dt.uint8
+FP8X4 = mybir.dt.float8_e4m3fn_x4
+ALU = mybir.AluOpType
+ACT = mybir.ActivationFunctionType
+
+P = 128
+SEQS = 3
+FRAMES = 1024
+CHANNELS = 512
+GROUPS = CHANNELS // P
+PACK = 4
+BANK = 512
+HALVES = FRAMES // BANK
+EPS = 1e-5
+VECTOR_COLS = 256
+
+FLOPS = 2 * SEQS * FRAMES * CHANNELS * CHANNELS
+
+
+def tile_transformerencoderblock_pa_kernel(tc, h_attn, x, masks, Wo, bo, out):
+    nc = tc.nc
+    with ExitStack() as ctx:
+        consts = ctx.enter_context(tc.tile_pool(name="consts", bufs=1))
+        inputs = ctx.enter_context(tc.tile_pool(name="inputs", bufs=1))
+        quant = ctx.enter_context(tc.tile_pool(name="quant", bufs=2))
+        work = ctx.enter_context(tc.tile_pool(name="work", bufs=3))
+        stats = ctx.enter_context(tc.tile_pool(name="stats", bufs=4))
+        transposed_psum = ctx.enter_context(tc.psum_pool(name="transposed_psum", bufs=3))
+        mask_psum = ctx.enter_context(tc.psum_pool(name="mask_psum", bufs=1))
+        product_psum = ctx.enter_context(tc.psum_pool(name="product_psum", bufs=4))
+
+        h_view = h_attn.rearrange("n (j r i) c -> n r j (i c)", r=P, i=2)
+        x_view = x.rearrange("n (p a) t -> n p a t", a=GROUPS)
+        out_view = out.rearrange("n (p a) t -> n p a t", a=GROUPS)
+
+        w_sb = consts.tile([P, GROUPS * CHANNELS], BF16)
+        nc.sync.dma_start(out=w_sb[:], in_=Wo.rearrange("(p a) c -> p (a c)", a=GROUPS))
+        h_sb = []
+        x_sb = []
+        for n in range(SEQS):
+            h_n = inputs.tile([P, FRAMES * CHANNELS // P], BF16, name="h_sb%d" % n)
+            x_n = inputs.tile([P, GROUPS, FRAMES], BF16, name="x_sb%d" % n)
+            for half in range(HALVES):
+                nc.sync.dma_start(
+                    out=h_n[:, half * 2048 : (half + 1) * 2048].rearrange("r (j c) -> r j c", j=2),
+                    in_=h_view[n][:, 2 * half : 2 * half + 2, :],
+                )
+            nc.sync.dma_start(out=x_n[:], in_=x_view[n])
+            h_sb.append(h_n)
+            x_sb.append(x_n)
+
+        ident = consts.tile([P, P], F32)
+        make_identity(nc, ident[:])
+        minus_half = consts.tile([P, 1], F32)
+        nc.gpsimd.memset(minus_half[:], -0.5)
+
+        mask_rows = consts.tile([P, SEQS * FRAMES], BF16)
+        nc.vector.memset(mask_rows[:], 0.0)
+        nc.scalar.dma_start(out=mask_rows[0:1, :], in_=masks.rearrange("n o t -> o (n t)"))
+        ones = consts.tile([P, P], BF16)
+        nc.vector.memset(ones[:], 1.0)
+        mask_sb = consts.tile([P, SEQS * FRAMES], BF16)
+
+        bo_sb = consts.tile([P, GROUPS], BF16)
+        nc.scalar.dma_start(out=bo_sb[:], in_=bo.rearrange("(p a) -> p a", a=GROUPS))
+        bias_f32 = consts.tile([P, GROUPS], F32)
+        nc.vector.tensor_copy(out=bias_f32[:], in_=bo_sb[:])
+
+        def broadcast_mask(n):
+            mask_ps = mask_psum.tile([P, FRAMES], BF16)
+            for half in range(HALVES):
+                nc.tensor.matmul(
+                    out=mask_ps[:, half * BANK : (half + 1) * BANK],
+                    lhsT=ones[:],
+                    rhs=mask_rows[:, n * FRAMES + half * BANK : n * FRAMES + (half + 1) * BANK],
+                    start=True,
+                    stop=True,
+                )
+            nc.scalar.copy(out=mask_sb[:, n * FRAMES : (n + 1) * FRAMES], in_=mask_ps[:])
+
+        w_words = w_sb[:].bitcast(F32)
+        w_grouped = consts.tile([P, GROUPS * P * PACK], BF16, align_bytes=64)
+        w_grouped_words = w_grouped[:].bitcast(F32)
+        w_codes = consts.tile([P, GROUPS * P], U32, align_bytes=64)
+        w_scales = consts.tile([P, GROUPS * P], U8, align_bytes=64)
+        for pair in range(GROUPS // 2):
+            w_ps = transposed_psum.tile([P, 2, 2, P], F32, tag="transposed")
+            for a2 in range(2):
+                for u in range(2):
+                    first_word = (2 * pair + a2) * 256 + u * P
+                    nc.tensor.transpose(
+                        w_ps[:, a2, u, :], w_words[:, first_word : first_word + P], ident[:]
+                    )
+            nc.vector.tensor_copy(
+                out=w_grouped_words[:, pair * BANK : (pair + 1) * BANK].rearrange(
+                    "q (a p u) -> q a p u", a=2, u=2
+                ),
+                in_=w_ps[:].rearrange("q a u p -> q a p u"),
+            )
+        nc.vector.quantize_mx(
+            out=w_codes[:].bitcast(FP8X4), scales=w_scales[:], in_=w_grouped[:]
+        )
+
+        def quantise_frames(n):
+            h_words = h_sb[n][:].bitcast(F32)
+            h_grouped = quant.tile([P, FRAMES * PACK], BF16, align_bytes=64)
+            h_grouped_words = h_grouped[:].bitcast(F32)
+            h_codes = quant.tile([P, FRAMES], U32, align_bytes=64)
+            h_scales = quant.tile([P, FRAMES], U8, align_bytes=64)
+            for half in range(HALVES):
+                for j in range(2 * half, 2 * half + 2):
+                    h_ps = transposed_psum.tile([P, 2, 2, P], F32, tag="transposed")
+                    for i in range(2):
+                        for u in range(2):
+                            first_word = j * 512 + i * 256 + u * P
+                            nc.tensor.transpose(
+                                h_ps[:, i, u, :], h_words[:, first_word : first_word + P], ident[:]
+                            )
+                    nc.scalar.copy(
+                        out=h_grouped_words[:, j * BANK : (j + 1) * BANK].rearrange(
+                            "q (r i u) -> q r i u", i=2, u=2
+                        ),
+                        in_=h_ps[:].rearrange("q i u r -> q r i u"),
+                    )
+                nc.vector.quantize_mx(
+                    out=h_codes[:, half * BANK : (half + 1) * BANK].bitcast(FP8X4),
+                    scales=h_scales[:, half * BANK : (half + 1) * BANK],
+                    in_=h_grouped[:, half * BANK * PACK : (half + 1) * BANK * PACK],
+                )
+            return h_codes, h_scales
+
+        def slab(n, a, h_codes, h_scales):
+            masked = work.tile([P, FRAMES], F32)
+            for half in range(HALVES):
+                cols = slice(half * BANK, (half + 1) * BANK)
+                product = product_psum.tile([P, BANK], F32)
+                nc.tensor.matmul_mx(
+                    out=product[:],
+                    lhsT=w_codes[:, a * P : (a + 1) * P].bitcast(FP8X4),
+                    lhsT_scale=w_scales[:, a * P : (a + 1) * P],
+                    rhs=h_codes[:, cols].bitcast(FP8X4),
+                    rhs_scale=h_scales[:, cols],
+                    start=True,
+                    stop=True,
+                )
+                nc.vector.scalar_tensor_tensor(
+                    out=masked[:, cols],
+                    in0=product[:],
+                    scalar=bias_f32[:, a : a + 1],
+                    in1=mask_sb[:, n * FRAMES + half * BANK : n * FRAMES + (half + 1) * BANK],
+                    op0=ALU.add,
+                    op1=ALU.mult,
+                )
+            y = work.tile([P, FRAMES], F32)
+            y_sum = stats.tile([P, 1], F32)
+            nc.vector.scalar_tensor_tensor(
+                out=y[:],
+                in0=masked[:],
+                scalar=1.0,
+                in1=x_sb[n][:, a, :],
+                op0=ALU.mult,
+                op1=ALU.add,
+                accum_out=y_sum[:],
+            )
+            neg_mean = stats.tile([P, 1], F32)
+            nc.gpsimd.tensor_scalar(
+                out=neg_mean[:], in0=y_sum[:], scalar1=-1.0 / FRAMES, scalar2=0.0,
+                op0=ALU.mult, op1=ALU.add,
+            )
+            squares = work.tile([P, FRAMES], BF16)
+            dev_sum = stats.tile([P, 1], F32)
+            nc.scalar.activation(
+                out=squares[:], in_=y[:], func=ACT.Square, bias=neg_mean[:], scale=1.0,
+                accum_out=dev_sum[:],
+            )
+            var_eps = stats.tile([P, 1], F32)
+            nc.gpsimd.tensor_scalar(
+                out=var_eps[:], in0=dev_sum[:], scalar1=1.0 / FRAMES, scalar2=EPS,
+                op0=ALU.mult, op1=ALU.add,
+            )
+            rstd = stats.tile([P, 1], F32)
+            nc.gpsimd.tensor_tensor(out=rstd[:], in0=var_eps[:], in1=minus_half[:], op=ALU.pow)
+            shift = stats.tile([P, 1], F32)
+            nc.gpsimd.tensor_tensor(out=shift[:], in0=neg_mean[:], in1=rstd[:], op=ALU.mult)
+            normed = work.tile([P, FRAMES], F32)
+            split = FRAMES - VECTOR_COLS
+            nc.scalar.activation(
+                out=normed[:, :split], in_=y[:, :split], func=ACT.Identity,
+                bias=shift[:], scale=rstd[:],
+            )
+            nc.vector.tensor_scalar(
+                out=normed[:, split:], in0=y[:, split:], scalar1=rstd[:], scalar2=shift[:],
+                op0=ALU.mult, op1=ALU.add,
+            )
+            nc.sync.dma_start(out=out_view[n][:, a, :], in_=normed[:])
+
+        broadcast_mask(0)
+        operands = quantise_frames(0)
+        for n in range(SEQS):
+            h_codes, h_scales = operands
+            for a in range(GROUPS):
+                slab(n, a, h_codes, h_scales)
+                if a == 0 and n + 1 < SEQS:
+                    broadcast_mask(n + 1)
+                    operands = quantise_frames(n + 1)

@@ -20,6 +20,7 @@ PACK = 4
 BANK = 512
 HALVES = FRAMES // BANK
 EPS = 1e-5
+SLABS = SEQS * GROUPS
 VECTOR_COLS = 256
 
 FLOPS = 2 * SEQS * FRAMES * CHANNELS * CHANNELS
@@ -31,48 +32,51 @@ def tile_transformerencoderblock_pa_kernel(tc, h_attn, x, masks, Wo, bo, out):
         consts = ctx.enter_context(tc.tile_pool(name="consts", bufs=1))
         inputs = ctx.enter_context(tc.tile_pool(name="inputs", bufs=1))
         quant = ctx.enter_context(tc.tile_pool(name="quant", bufs=2))
-        work = ctx.enter_context(tc.tile_pool(name="work", bufs=3))
+        scratch = ctx.enter_context(tc.tile_pool(name="scratch", bufs=2))
+        slabs = ctx.enter_context(tc.tile_pool(name="slabs", bufs=4))
         stats = ctx.enter_context(tc.tile_pool(name="stats", bufs=4))
         transposed_psum = ctx.enter_context(tc.psum_pool(name="transposed_psum", bufs=3))
         mask_psum = ctx.enter_context(tc.psum_pool(name="mask_psum", bufs=1))
         product_psum = ctx.enter_context(tc.psum_pool(name="product_psum", bufs=4))
+        ctx.enter_context(tc.manual_schedule())
 
         h_view = h_attn.rearrange("n (j r i) c -> n r j (i c)", r=P, i=2)
         x_view = x.rearrange("n (p a) t -> n p a t", a=GROUPS)
         out_view = out.rearrange("n (p a) t -> n p a t", a=GROUPS)
 
-        w_sb = consts.tile([P, GROUPS * CHANNELS], BF16)
-        nc.sync.dma_start(out=w_sb[:], in_=Wo.rearrange("(p a) c -> p (a c)", a=GROUPS))
-        h_sb = []
-        x_sb = []
-        for n in range(SEQS):
-            h_n = inputs.tile([P, FRAMES * CHANNELS // P], BF16, name="h_sb%d" % n)
-            x_n = inputs.tile([P, GROUPS, FRAMES], BF16, name="x_sb%d" % n)
-            for half in range(HALVES):
-                nc.sync.dma_start(
-                    out=h_n[:, half * 2048 : (half + 1) * 2048].rearrange("r (j c) -> r j c", j=2),
-                    in_=h_view[n][:, 2 * half : 2 * half + 2, :],
-                )
-            nc.sync.dma_start(out=x_n[:], in_=x_view[n])
-            h_sb.append(h_n)
-            x_sb.append(x_n)
-
         ident = consts.tile([P, P], F32)
         make_identity(nc, ident[:])
         minus_half = consts.tile([P, 1], F32)
         nc.gpsimd.memset(minus_half[:], -0.5)
-
         mask_rows = consts.tile([P, SEQS * FRAMES], BF16)
         nc.vector.memset(mask_rows[:], 0.0)
-        nc.scalar.dma_start(out=mask_rows[0:1, :], in_=masks.rearrange("n o t -> o (n t)"))
         ones = consts.tile([P, P], BF16)
         nc.vector.memset(ones[:], 1.0)
         mask_sb = consts.tile([P, SEQS * FRAMES], BF16)
 
+        w_sb = consts.tile([P, GROUPS * CHANNELS], BF16)
         bo_sb = consts.tile([P, GROUPS], BF16)
-        nc.scalar.dma_start(out=bo_sb[:], in_=bo.rearrange("(p a) -> p a", a=GROUPS))
-        bias_f32 = consts.tile([P, GROUPS], F32)
-        nc.vector.tensor_copy(out=bias_f32[:], in_=bo_sb[:])
+        h_sb = [
+            inputs.tile([P, FRAMES * CHANNELS // P], BF16, name="h_sb%d" % n) for n in range(SEQS)
+        ]
+        x_sb = [inputs.tile([P, GROUPS, FRAMES], BF16, name="x_sb%d" % n) for n in range(SEQS)]
+
+        def load_frames(n, half):
+            nc.sync.dma_start(
+                out=h_sb[n][:, half * 2048 : (half + 1) * 2048].rearrange("r (j c) -> r j c", j=2),
+                in_=h_view[n][:, 2 * half : 2 * half + 2, :],
+            )
+
+        nc.sync.dma_start(out=w_sb[:], in_=Wo.rearrange("(p a) c -> p (a c)", a=GROUPS))
+        load_frames(0, 0)
+        nc.sync.dma_start(out=mask_rows[0:1, :], in_=masks.rearrange("n o t -> o (n t)"))
+        nc.sync.dma_start(out=bo_sb[:], in_=bo.rearrange("(p a) -> p a", a=GROUPS))
+        load_frames(0, 1)
+        nc.sync.dma_start(out=x_sb[0][:], in_=x_view[0])
+        for n in range(1, SEQS):
+            load_frames(n, 0)
+            load_frames(n, 1)
+            nc.sync.dma_start(out=x_sb[n][:], in_=x_view[n])
 
         def broadcast_mask(n):
             mask_ps = mask_psum.tile([P, FRAMES], BF16)
@@ -84,7 +88,7 @@ def tile_transformerencoderblock_pa_kernel(tc, h_attn, x, masks, Wo, bo, out):
                     start=True,
                     stop=True,
                 )
-            nc.scalar.copy(out=mask_sb[:, n * FRAMES : (n + 1) * FRAMES], in_=mask_ps[:])
+            nc.vector.tensor_copy(out=mask_sb[:, n * FRAMES : (n + 1) * FRAMES], in_=mask_ps[:])
 
         w_words = w_sb[:].bitcast(F32)
         w_grouped = consts.tile([P, GROUPS * P * PACK], BF16, align_bytes=64)
@@ -99,46 +103,55 @@ def tile_transformerencoderblock_pa_kernel(tc, h_attn, x, masks, Wo, bo, out):
                     nc.tensor.transpose(
                         w_ps[:, a2, u, :], w_words[:, first_word : first_word + P], ident[:]
                     )
-            nc.vector.tensor_copy(
-                out=w_grouped_words[:, pair * BANK : (pair + 1) * BANK].rearrange(
-                    "q (a p u) -> q a p u", a=2, u=2
-                ),
-                in_=w_ps[:].rearrange("q a u p -> q a p u"),
+            regrouped = w_grouped_words[:, pair * BANK : (pair + 1) * BANK].rearrange(
+                "q (a p u) -> q a p u", a=2, u=2
             )
+            if pair == 0:
+                nc.vector.tensor_copy(out=regrouped, in_=w_ps[:].rearrange("q a u p -> q a p u"))
+            else:
+                nc.scalar.copy(out=regrouped, in_=w_ps[:].rearrange("q a u p -> q a p u"))
         nc.vector.quantize_mx(
             out=w_codes[:].bitcast(FP8X4), scales=w_scales[:], in_=w_grouped[:]
         )
 
-        def quantise_frames(n):
-            h_words = h_sb[n][:].bitcast(F32)
-            h_grouped = quant.tile([P, FRAMES * PACK], BF16, align_bytes=64)
-            h_grouped_words = h_grouped[:].bitcast(F32)
-            h_codes = quant.tile([P, FRAMES], U32, align_bytes=64)
-            h_scales = quant.tile([P, FRAMES], U8, align_bytes=64)
-            for half in range(HALVES):
-                for j in range(2 * half, 2 * half + 2):
-                    h_ps = transposed_psum.tile([P, 2, 2, P], F32, tag="transposed")
-                    for i in range(2):
-                        for u in range(2):
-                            first_word = j * 512 + i * 256 + u * P
-                            nc.tensor.transpose(
-                                h_ps[:, i, u, :], h_words[:, first_word : first_word + P], ident[:]
-                            )
-                    nc.scalar.copy(
-                        out=h_grouped_words[:, j * BANK : (j + 1) * BANK].rearrange(
-                            "q (r i u) -> q r i u", i=2, u=2
-                        ),
-                        in_=h_ps[:].rearrange("q i u r -> q r i u"),
-                    )
-                nc.vector.quantize_mx(
-                    out=h_codes[:, half * BANK : (half + 1) * BANK].bitcast(FP8X4),
-                    scales=h_scales[:, half * BANK : (half + 1) * BANK],
-                    in_=h_grouped[:, half * BANK * PACK : (half + 1) * BANK * PACK],
-                )
-            return h_codes, h_scales
+        frames = {}
 
-        def slab(n, a, h_codes, h_scales):
-            masked = work.tile([P, FRAMES], F32)
+        def transpose_quarter(n, j):
+            if j == 0:
+                h_grouped = quant.tile([P, FRAMES * PACK], BF16, align_bytes=64)
+                h_codes = quant.tile([P, FRAMES], U32, align_bytes=64)
+                h_scales = quant.tile([P, FRAMES], U8, align_bytes=64)
+                frames[n] = (h_grouped, h_codes, h_scales)
+            h_words = h_sb[n][:].bitcast(F32)
+            h_ps = transposed_psum.tile([P, 2, 2, P], F32, tag="transposed")
+            for i in range(2):
+                for u in range(2):
+                    first_word = j * 512 + i * 256 + u * P
+                    nc.tensor.transpose(
+                        h_ps[:, i, u, :], h_words[:, first_word : first_word + P], ident[:]
+                    )
+            nc.scalar.copy(
+                out=frames[n][0][:].bitcast(F32)[:, j * BANK : (j + 1) * BANK].rearrange(
+                    "q (r i u) -> q r i u", i=2, u=2
+                ),
+                in_=h_ps[:].rearrange("q i u r -> q r i u"),
+            )
+
+        def quantise_half(n, half):
+            h_grouped, h_codes, h_scales = frames[n]
+            nc.vector.quantize_mx(
+                out=h_codes[:, half * BANK : (half + 1) * BANK].bitcast(FP8X4),
+                scales=h_scales[:, half * BANK : (half + 1) * BANK],
+                in_=h_grouped[:, half * BANK * PACK : (half + 1) * BANK * PACK],
+            )
+
+        summed = {}
+        scaled = {}
+
+        def project_and_add(k):
+            n, a = divmod(k, GROUPS)
+            h_codes, h_scales = frames[n][1:]
+            masked = scratch.tile([P, FRAMES], F32)
             for half in range(HALVES):
                 cols = slice(half * BANK, (half + 1) * BANK)
                 product = product_psum.tile([P, BANK], F32)
@@ -159,7 +172,7 @@ def tile_transformerencoderblock_pa_kernel(tc, h_attn, x, masks, Wo, bo, out):
                     op0=ALU.add,
                     op1=ALU.mult,
                 )
-            y = work.tile([P, FRAMES], F32)
+            y = slabs.tile([P, FRAMES], F32)
             y_sum = stats.tile([P, 1], F32)
             nc.vector.scalar_tensor_tensor(
                 out=y[:],
@@ -170,27 +183,35 @@ def tile_transformerencoderblock_pa_kernel(tc, h_attn, x, masks, Wo, bo, out):
                 op1=ALU.add,
                 accum_out=y_sum[:],
             )
-            neg_mean = stats.tile([P, 1], F32)
-            nc.gpsimd.tensor_scalar(
-                out=neg_mean[:], in0=y_sum[:], scalar1=-1.0 / FRAMES, scalar2=0.0,
-                op0=ALU.mult, op1=ALU.add,
-            )
-            squares = work.tile([P, FRAMES], BF16)
+            summed[k] = (y, y_sum)
+
+        def deviation(k):
+            y, y_sum = summed[k]
+            squares = scratch.tile([P, FRAMES], BF16)
             dev_sum = stats.tile([P, 1], F32)
             nc.scalar.activation(
-                out=squares[:], in_=y[:], func=ACT.Square, bias=neg_mean[:], scale=1.0,
+                out=squares[:], in_=y[:], func=ACT.Square, bias=y_sum[:], scale=-float(FRAMES),
                 accum_out=dev_sum[:],
             )
             var_eps = stats.tile([P, 1], F32)
             nc.gpsimd.tensor_scalar(
-                out=var_eps[:], in0=dev_sum[:], scalar1=1.0 / FRAMES, scalar2=EPS,
+                out=var_eps[:], in0=dev_sum[:], scalar1=1.0 / FRAMES**3, scalar2=EPS,
                 op0=ALU.mult, op1=ALU.add,
             )
             rstd = stats.tile([P, 1], F32)
             nc.gpsimd.tensor_tensor(out=rstd[:], in0=var_eps[:], in1=minus_half[:], op=ALU.pow)
             shift = stats.tile([P, 1], F32)
-            nc.gpsimd.tensor_tensor(out=shift[:], in0=neg_mean[:], in1=rstd[:], op=ALU.mult)
-            normed = work.tile([P, FRAMES], F32)
+            nc.gpsimd.tensor_scalar(
+                out=shift[:], in0=y_sum[:], scalar1=rstd[:], scalar2=-1.0 / FRAMES,
+                op0=ALU.mult, op1=ALU.mult,
+            )
+            scaled[k] = (rstd, shift)
+
+        def normalise_and_store(k):
+            n, a = divmod(k, GROUPS)
+            y = summed[k][0]
+            rstd, shift = scaled[k]
+            normed = slabs.tile([P, FRAMES], F32)
             split = FRAMES - VECTOR_COLS
             nc.scalar.activation(
                 out=normed[:, :split], in_=y[:, :split], func=ACT.Identity,
@@ -202,12 +223,27 @@ def tile_transformerencoderblock_pa_kernel(tc, h_attn, x, masks, Wo, bo, out):
             )
             nc.sync.dma_start(out=out_view[n][:, a, :], in_=normed[:])
 
-        broadcast_mask(0)
-        operands = quantise_frames(0)
-        for n in range(SEQS):
-            h_codes, h_scales = operands
-            for a in range(GROUPS):
-                slab(n, a, h_codes, h_scales)
-                if a == 0 and n + 1 < SEQS:
-                    broadcast_mask(n + 1)
-                    operands = quantise_frames(n + 1)
+        for j in range(GROUPS):
+            transpose_quarter(0, j)
+            if j == 1:
+                broadcast_mask(0)
+            if j % 2 == 1:
+                quantise_half(0, j // 2)
+        bias_f32 = consts.tile([P, GROUPS], F32)
+        nc.vector.tensor_copy(out=bias_f32[:], in_=bo_sb[:])
+
+        for k in range(SLABS + 2):
+            n, a = divmod(k, GROUPS)
+            prepare = n + 1 < SEQS
+            if 1 <= k <= SLABS:
+                deviation(k - 1)
+            if k < SLABS:
+                project_and_add(k)
+            if prepare:
+                transpose_quarter(n + 1, a)
+            if prepare and a % 2 == 1:
+                quantise_half(n + 1, a // 2)
+            if prepare and a == 2:
+                broadcast_mask(n + 1)
+            if k >= 2:
+                normalise_and_store(k - 2)

@@ -21,7 +21,7 @@ BANK = 512
 HALVES = FRAMES // BANK
 EPS = 1e-5
 SLABS = SEQS * GROUPS
-VECTOR_COLS = 256
+VECTOR_COLS = 192
 
 FLOPS = 2 * SEQS * FRAMES * CHANNELS * CHANNELS
 
@@ -32,7 +32,7 @@ def tile_transformerencoderblock_pa_kernel(tc, h_attn, x, masks, Wo, bo, out):
         consts = ctx.enter_context(tc.tile_pool(name="consts", bufs=1))
         inputs = ctx.enter_context(tc.tile_pool(name="inputs", bufs=1))
         quant = ctx.enter_context(tc.tile_pool(name="quant", bufs=2))
-        scratch = ctx.enter_context(tc.tile_pool(name="scratch", bufs=2))
+        scratch = ctx.enter_context(tc.tile_pool(name="scratch", bufs=3))
         slabs = ctx.enter_context(tc.tile_pool(name="slabs", bufs=4))
         stats = ctx.enter_context(tc.tile_pool(name="stats", bufs=4))
         transposed_psum = ctx.enter_context(tc.psum_pool(name="transposed_psum", bufs=3))
@@ -88,7 +88,7 @@ def tile_transformerencoderblock_pa_kernel(tc, h_attn, x, masks, Wo, bo, out):
                     start=True,
                     stop=True,
                 )
-            nc.vector.tensor_copy(out=mask_sb[:, n * FRAMES : (n + 1) * FRAMES], in_=mask_ps[:])
+            nc.scalar.copy(out=mask_sb[:, n * FRAMES : (n + 1) * FRAMES], in_=mask_ps[:])
 
         w_words = w_sb[:].bitcast(F32)
         w_grouped = consts.tile([P, GROUPS * P * PACK], BF16, align_bytes=64)
@@ -116,7 +116,7 @@ def tile_transformerencoderblock_pa_kernel(tc, h_attn, x, masks, Wo, bo, out):
 
         frames = {}
 
-        def transpose_quarter(n, j):
+        def transpose_quarter(n, j, on_vector=False):
             if j == 0:
                 h_grouped = quant.tile([P, FRAMES * PACK], BF16, align_bytes=64)
                 h_codes = quant.tile([P, FRAMES], U32, align_bytes=64)
@@ -130,12 +130,13 @@ def tile_transformerencoderblock_pa_kernel(tc, h_attn, x, masks, Wo, bo, out):
                     nc.tensor.transpose(
                         h_ps[:, i, u, :], h_words[:, first_word : first_word + P], ident[:]
                     )
-            nc.scalar.copy(
-                out=frames[n][0][:].bitcast(F32)[:, j * BANK : (j + 1) * BANK].rearrange(
-                    "q (r i u) -> q r i u", i=2, u=2
-                ),
-                in_=h_ps[:].rearrange("q i u r -> q r i u"),
+            regrouped = frames[n][0][:].bitcast(F32)[:, j * BANK : (j + 1) * BANK].rearrange(
+                "q (r i u) -> q r i u", i=2, u=2
             )
+            if on_vector:
+                nc.vector.tensor_copy(out=regrouped, in_=h_ps[:].rearrange("q i u r -> q r i u"))
+            else:
+                nc.scalar.copy(out=regrouped, in_=h_ps[:].rearrange("q i u r -> q r i u"))
 
         def quantise_half(n, half):
             h_grouped, h_codes, h_scales = frames[n]
@@ -145,10 +146,11 @@ def tile_transformerencoderblock_pa_kernel(tc, h_attn, x, masks, Wo, bo, out):
                 in_=h_grouped[:, half * BANK * PACK : (half + 1) * BANK * PACK],
             )
 
+        projected = {}
         summed = {}
         scaled = {}
 
-        def project_and_add(k):
+        def project(k):
             n, a = divmod(k, GROUPS)
             h_codes, h_scales = frames[n][1:]
             masked = scratch.tile([P, FRAMES], F32)
@@ -172,6 +174,11 @@ def tile_transformerencoderblock_pa_kernel(tc, h_attn, x, masks, Wo, bo, out):
                     op0=ALU.add,
                     op1=ALU.mult,
                 )
+            projected[k] = masked
+
+        def add_residual(k):
+            n, a = divmod(k, GROUPS)
+            masked = projected[k]
             y = slabs.tile([P, FRAMES], F32)
             y_sum = stats.tile([P, 1], F32)
             nc.vector.scalar_tensor_tensor(
@@ -224,26 +231,27 @@ def tile_transformerencoderblock_pa_kernel(tc, h_attn, x, masks, Wo, bo, out):
             nc.sync.dma_start(out=out_view[n][:, a, :], in_=normed[:])
 
         for j in range(GROUPS):
-            transpose_quarter(0, j)
-            if j == 1:
-                broadcast_mask(0)
+            transpose_quarter(0, j, on_vector=(j % 2 == 1))
             if j % 2 == 1:
                 quantise_half(0, j // 2)
+        broadcast_mask(0)
         bias_f32 = consts.tile([P, GROUPS], F32)
         nc.vector.tensor_copy(out=bias_f32[:], in_=bo_sb[:])
 
-        for k in range(SLABS + 2):
+        for k in range(SLABS + 3):
             n, a = divmod(k, GROUPS)
             prepare = n + 1 < SEQS
-            if 1 <= k <= SLABS:
-                deviation(k - 1)
+            if 2 <= k < SLABS + 2:
+                deviation(k - 2)
             if k < SLABS:
-                project_and_add(k)
+                project(k)
+            if 1 <= k < SLABS + 1:
+                add_residual(k - 1)
             if prepare:
                 transpose_quarter(n + 1, a)
             if prepare and a % 2 == 1:
                 quantise_half(n + 1, a // 2)
             if prepare and a == 2:
                 broadcast_mask(n + 1)
-            if k >= 2:
-                normalise_and_store(k - 2)
+            if k >= 3:
+                normalise_and_store(k - 3)

@@ -21,7 +21,8 @@ BANK = 512
 HALVES = FRAMES // BANK
 EPS = 1e-5
 SLABS = SEQS * GROUPS
-VECTOR_COLS = 192
+VECTOR_COLS = 128
+DRAIN_VECTOR_COLS = 640
 
 FLOPS = 2 * SEQS * FRAMES * CHANNELS * CHANNELS
 
@@ -31,7 +32,7 @@ def tile_transformerencoderblock_pa_kernel(tc, h_attn, x, masks, Wo, bo, out):
     with ExitStack() as ctx:
         consts = ctx.enter_context(tc.tile_pool(name="consts", bufs=1))
         inputs = ctx.enter_context(tc.tile_pool(name="inputs", bufs=1))
-        quant = ctx.enter_context(tc.tile_pool(name="quant", bufs=2))
+        quant = ctx.enter_context(tc.tile_pool(name="quant", bufs=SEQS))
         scratch = ctx.enter_context(tc.tile_pool(name="scratch", bufs=3))
         slabs = ctx.enter_context(tc.tile_pool(name="slabs", bufs=4))
         stats = ctx.enter_context(tc.tile_pool(name="stats", bufs=4))
@@ -76,6 +77,7 @@ def tile_transformerencoderblock_pa_kernel(tc, h_attn, x, masks, Wo, bo, out):
         for n in range(1, SEQS):
             load_frames(n, 0)
             load_frames(n, 1)
+        for n in range(1, SEQS):
             nc.sync.dma_start(out=x_sb[n][:], in_=x_view[n])
 
         def broadcast_mask(n):
@@ -214,12 +216,12 @@ def tile_transformerencoderblock_pa_kernel(tc, h_attn, x, masks, Wo, bo, out):
             )
             scaled[k] = (rstd, shift)
 
-        def normalise_and_store(k):
+        def normalise_and_store(k, vector_cols):
             n, a = divmod(k, GROUPS)
             y = summed[k][0]
             rstd, shift = scaled[k]
             normed = slabs.tile([P, FRAMES], F32)
-            split = FRAMES - VECTOR_COLS
+            split = FRAMES - vector_cols
             nc.scalar.activation(
                 out=normed[:, :split], in_=y[:, :split], func=ACT.Identity,
                 bias=shift[:], scale=rstd[:],
@@ -239,19 +241,20 @@ def tile_transformerencoderblock_pa_kernel(tc, h_attn, x, masks, Wo, bo, out):
         nc.vector.tensor_copy(out=bias_f32[:], in_=bo_sb[:])
 
         for k in range(SLABS + 3):
-            n, a = divmod(k, GROUPS)
-            prepare = n + 1 < SEQS
             if 2 <= k < SLABS + 2:
                 deviation(k - 2)
             if k < SLABS:
                 project(k)
             if 1 <= k < SLABS + 1:
                 add_residual(k - 1)
-            if prepare:
-                transpose_quarter(n + 1, a)
-            if prepare and a % 2 == 1:
-                quantise_half(n + 1, a // 2)
-            if prepare and a == 2:
-                broadcast_mask(n + 1)
+            if 1 <= k <= (SEQS - 1) * HALVES:
+                n, half = divmod(k + 1, HALVES)
+                transpose_quarter(n, 2 * half)
+                transpose_quarter(n, 2 * half + 1)
+            if 2 <= k <= (SEQS - 1) * HALVES + 1:
+                n, half = divmod(k, HALVES)
+                quantise_half(n, half)
+            if 1 <= k < SEQS:
+                broadcast_mask(k)
             if k >= 3:
-                normalise_and_store(k - 3)
+                normalise_and_store(k - 3, VECTOR_COLS if k <= SLABS else DRAIN_VECTOR_COLS)

@@ -21,8 +21,7 @@ BANK = 512
 HALVES = FRAMES // BANK
 EPS = 1e-5
 SLABS = SEQS * GROUPS
-VECTOR_COLS = 128
-DRAIN_VECTOR_COLS = 640
+VECTOR_EVERY = 3
 
 FLOPS = 2 * SEQS * FRAMES * CHANNELS * CHANNELS
 
@@ -216,20 +215,20 @@ def tile_transformerencoderblock_pa_kernel(tc, h_attn, x, masks, Wo, bo, out):
             )
             scaled[k] = (rstd, shift)
 
-        def normalise_and_store(k, vector_cols):
+        def normalise_and_store(k):
             n, a = divmod(k, GROUPS)
             y = summed[k][0]
             rstd, shift = scaled[k]
             normed = slabs.tile([P, FRAMES], F32)
-            split = FRAMES - vector_cols
-            nc.scalar.activation(
-                out=normed[:, :split], in_=y[:, :split], func=ACT.Identity,
-                bias=shift[:], scale=rstd[:],
-            )
-            nc.vector.tensor_scalar(
-                out=normed[:, split:], in0=y[:, split:], scalar1=rstd[:], scalar2=shift[:],
-                op0=ALU.mult, op1=ALU.add,
-            )
+            if k % VECTOR_EVERY == VECTOR_EVERY - 1:
+                nc.vector.tensor_scalar(
+                    out=normed[:], in0=y[:], scalar1=rstd[:], scalar2=shift[:],
+                    op0=ALU.mult, op1=ALU.add,
+                )
+            else:
+                nc.scalar.activation(
+                    out=normed[:], in_=y[:], func=ACT.Identity, bias=shift[:], scale=rstd[:]
+                )
             nc.sync.dma_start(out=out_view[n][:, a, :], in_=normed[:])
 
         for j in range(GROUPS):
@@ -257,4 +256,4 @@ def tile_transformerencoderblock_pa_kernel(tc, h_attn, x, masks, Wo, bo, out):
             if 1 <= k < SEQS:
                 broadcast_mask(k)
             if k >= 3:
-                normalise_and_store(k - 3, VECTOR_COLS if k <= SLABS else DRAIN_VECTOR_COLS)
+                normalise_and_store(k - 3)

from contextlib import ExitStack

import concourse.mybir as mybir
from concourse.masks import make_identity

F32 = mybir.dt.float32
BF16 = mybir.dt.bfloat16
U32 = mybir.dt.uint32
U8 = mybir.dt.uint8
FP8X4 = mybir.dt.float8_e4m3fn_x4
ALU = mybir.AluOpType
ACT = mybir.ActivationFunctionType

P = 128
SEQS = 3
FRAMES = 1024
CHANNELS = 512
GROUPS = CHANNELS // P
PACK = 4
BANK = 512
HALVES = FRAMES // BANK
EPS = 1e-5
SLABS = SEQS * GROUPS
VECTOR_EVERY = 3

FLOPS = 2 * SEQS * FRAMES * CHANNELS * CHANNELS


def tile_transformerencoderblock_pa_kernel(tc, h_attn, x, masks, Wo, bo, out):
    nc = tc.nc
    with ExitStack() as ctx:
        consts = ctx.enter_context(tc.tile_pool(name="consts", bufs=1))
        inputs = ctx.enter_context(tc.tile_pool(name="inputs", bufs=1))
        quant = ctx.enter_context(tc.tile_pool(name="quant", bufs=SEQS))
        scratch = ctx.enter_context(tc.tile_pool(name="scratch", bufs=3))
        slabs = ctx.enter_context(tc.tile_pool(name="slabs", bufs=4))
        stats = ctx.enter_context(tc.tile_pool(name="stats", bufs=4))
        transposed_psum = ctx.enter_context(tc.psum_pool(name="transposed_psum", bufs=3))
        mask_psum = ctx.enter_context(tc.psum_pool(name="mask_psum", bufs=1))
        product_psum = ctx.enter_context(tc.psum_pool(name="product_psum", bufs=4))
        ctx.enter_context(tc.manual_schedule())

        h_view = h_attn.rearrange("n (j r i) c -> n r j (i c)", r=P, i=2)
        x_view = x.rearrange("n (p a) t -> n p a t", a=GROUPS)
        out_view = out.rearrange("n (p a) t -> n p a t", a=GROUPS)

        ident = consts.tile([P, P], F32)
        make_identity(nc, ident[:])
        minus_half = consts.tile([P, 1], F32)
        nc.gpsimd.memset(minus_half[:], -0.5)
        mask_rows = consts.tile([P, SEQS * FRAMES], BF16)
        nc.vector.memset(mask_rows[:], 0.0)
        ones = consts.tile([P, P], BF16)
        nc.vector.memset(ones[:], 1.0)
        mask_sb = consts.tile([P, SEQS * FRAMES], BF16)

        w_sb = consts.tile([P, GROUPS * CHANNELS], BF16)
        bo_sb = consts.tile([P, GROUPS], BF16)
        h_sb = [
            inputs.tile([P, FRAMES * CHANNELS // P], BF16, name="h_sb%d" % n) for n in range(SEQS)
        ]
        x_sb = [inputs.tile([P, GROUPS, FRAMES], BF16, name="x_sb%d" % n) for n in range(SEQS)]

        def load_frames(n, half):
            nc.sync.dma_start(
                out=h_sb[n][:, half * 2048 : (half + 1) * 2048].rearrange("r (j c) -> r j c", j=2),
                in_=h_view[n][:, 2 * half : 2 * half + 2, :],
            )

        nc.sync.dma_start(out=w_sb[:], in_=Wo.rearrange("(p a) c -> p (a c)", a=GROUPS))
        load_frames(0, 0)
        nc.sync.dma_start(out=mask_rows[0:1, :], in_=masks.rearrange("n o t -> o (n t)"))
        nc.sync.dma_start(out=bo_sb[:], in_=bo.rearrange("(p a) -> p a", a=GROUPS))
        load_frames(0, 1)
        nc.sync.dma_start(out=x_sb[0][:], in_=x_view[0])
        for n in range(1, SEQS):
            load_frames(n, 0)
            load_frames(n, 1)
        for n in range(1, SEQS):
            nc.sync.dma_start(out=x_sb[n][:], in_=x_view[n])

        def broadcast_mask(n):
            mask_ps = mask_psum.tile([P, FRAMES], BF16)
            for half in range(HALVES):
                nc.tensor.matmul(
                    out=mask_ps[:, half * BANK : (half + 1) * BANK],
                    lhsT=ones[:],
                    rhs=mask_rows[:, n * FRAMES + half * BANK : n * FRAMES + (half + 1) * BANK],
                    start=True,
                    stop=True,
                )
            nc.scalar.copy(out=mask_sb[:, n * FRAMES : (n + 1) * FRAMES], in_=mask_ps[:])

        w_words = w_sb[:].bitcast(F32)
        w_grouped = consts.tile([P, GROUPS * P * PACK], BF16, align_bytes=64)
        w_grouped_words = w_grouped[:].bitcast(F32)
        w_codes = consts.tile([P, GROUPS * P], U32, align_bytes=64)
        w_scales = consts.tile([P, GROUPS * P], U8, align_bytes=64)
        for pair in range(GROUPS // 2):
            w_ps = transposed_psum.tile([P, 2, 2, P], F32, tag="transposed")
            for a2 in range(2):
                for u in range(2):
                    first_word = (2 * pair + a2) * 256 + u * P
                    nc.tensor.transpose(
                        w_ps[:, a2, u, :], w_words[:, first_word : first_word + P], ident[:]
                    )
            regrouped = w_grouped_words[:, pair * BANK : (pair + 1) * BANK].rearrange(
                "q (a p u) -> q a p u", a=2, u=2
            )
            if pair == 0:
                nc.vector.tensor_copy(out=regrouped, in_=w_ps[:].rearrange("q a u p -> q a p u"))
            else:
                nc.scalar.copy(out=regrouped, in_=w_ps[:].rearrange("q a u p -> q a p u"))
        nc.vector.quantize_mx(
            out=w_codes[:].bitcast(FP8X4), scales=w_scales[:], in_=w_grouped[:]
        )

        frames = {}

        def transpose_quarter(n, j, on_vector=False):
            if j == 0:
                h_grouped = quant.tile([P, FRAMES * PACK], BF16, align_bytes=64)
                h_codes = quant.tile([P, FRAMES], U32, align_bytes=64)
                h_scales = quant.tile([P, FRAMES], U8, align_bytes=64)
                frames[n] = (h_grouped, h_codes, h_scales)
            h_words = h_sb[n][:].bitcast(F32)
            h_ps = transposed_psum.tile([P, 2, 2, P], F32, tag="transposed")
            for i in range(2):
                for u in range(2):
                    first_word = j * 512 + i * 256 + u * P
                    nc.tensor.transpose(
                        h_ps[:, i, u, :], h_words[:, first_word : first_word + P], ident[:]
                    )
            regrouped = frames[n][0][:].bitcast(F32)[:, j * BANK : (j + 1) * BANK].rearrange(
                "q (r i u) -> q r i u", i=2, u=2
            )
            if on_vector:
                nc.vector.tensor_copy(out=regrouped, in_=h_ps[:].rearrange("q i u r -> q r i u"))
            else:
                nc.scalar.copy(out=regrouped, in_=h_ps[:].rearrange("q i u r -> q r i u"))

        def quantise_half(n, half):
            h_grouped, h_codes, h_scales = frames[n]
            nc.vector.quantize_mx(
                out=h_codes[:, half * BANK : (half + 1) * BANK].bitcast(FP8X4),
                scales=h_scales[:, half * BANK : (half + 1) * BANK],
                in_=h_grouped[:, half * BANK * PACK : (half + 1) * BANK * PACK],
            )

        projected = {}
        summed = {}
        scaled = {}

        def project(k):
            n, a = divmod(k, GROUPS)
            h_codes, h_scales = frames[n][1:]
            masked = scratch.tile([P, FRAMES], F32)
            for half in range(HALVES):
                cols = slice(half * BANK, (half + 1) * BANK)
                product = product_psum.tile([P, BANK], F32)
                nc.tensor.matmul_mx(
                    out=product[:],
                    lhsT=w_codes[:, a * P : (a + 1) * P].bitcast(FP8X4),
                    lhsT_scale=w_scales[:, a * P : (a + 1) * P],
                    rhs=h_codes[:, cols].bitcast(FP8X4),
                    rhs_scale=h_scales[:, cols],
                    start=True,
                    stop=True,
                )
                nc.vector.scalar_tensor_tensor(
                    out=masked[:, cols],
                    in0=product[:],
                    scalar=bias_f32[:, a : a + 1],
                    in1=mask_sb[:, n * FRAMES + half * BANK : n * FRAMES + (half + 1) * BANK],
                    op0=ALU.add,
                    op1=ALU.mult,
                )
            projected[k] = masked

        def add_residual(k):
            n, a = divmod(k, GROUPS)
            masked = projected[k]
            y = slabs.tile([P, FRAMES], F32)
            y_sum = stats.tile([P, 1], F32)
            nc.vector.scalar_tensor_tensor(
                out=y[:],
                in0=masked[:],
                scalar=1.0,
                in1=x_sb[n][:, a, :],
                op0=ALU.mult,
                op1=ALU.add,
                accum_out=y_sum[:],
            )
            summed[k] = (y, y_sum)

        def deviation(k):
            y, y_sum = summed[k]
            squares = scratch.tile([P, FRAMES], BF16)
            dev_sum = stats.tile([P, 1], F32)
            nc.scalar.activation(
                out=squares[:], in_=y[:], func=ACT.Square, bias=y_sum[:], scale=-float(FRAMES),
                accum_out=dev_sum[:],
            )
            var_eps = stats.tile([P, 1], F32)
            nc.gpsimd.tensor_scalar(
                out=var_eps[:], in0=dev_sum[:], scalar1=1.0 / FRAMES**3, scalar2=EPS,
                op0=ALU.mult, op1=ALU.add,
            )
            rstd = stats.tile([P, 1], F32)
            nc.gpsimd.tensor_tensor(out=rstd[:], in0=var_eps[:], in1=minus_half[:], op=ALU.pow)
            shift = stats.tile([P, 1], F32)
            nc.gpsimd.tensor_scalar(
                out=shift[:], in0=y_sum[:], scalar1=rstd[:], scalar2=-1.0 / FRAMES,
                op0=ALU.mult, op1=ALU.mult,
            )
            scaled[k] = (rstd, shift)

        def normalise_and_store(k):
            n, a = divmod(k, GROUPS)
            y = summed[k][0]
            rstd, shift = scaled[k]
            normed = slabs.tile([P, FRAMES], F32)
            if k % VECTOR_EVERY == VECTOR_EVERY - 1:
                nc.vector.tensor_scalar(
                    out=normed[:], in0=y[:], scalar1=rstd[:], scalar2=shift[:],
                    op0=ALU.mult, op1=ALU.add,
                )
            else:
                nc.scalar.activation(
                    out=normed[:], in_=y[:], func=ACT.Identity, bias=shift[:], scale=rstd[:]
                )
            nc.sync.dma_start(out=out_view[n][:, a, :], in_=normed[:])

        for j in range(GROUPS):
            transpose_quarter(0, j, on_vector=(j % 2 == 1))
            if j % 2 == 1:
                quantise_half(0, j // 2)
        broadcast_mask(0)
        bias_f32 = consts.tile([P, GROUPS], F32)
        nc.vector.tensor_copy(out=bias_f32[:], in_=bo_sb[:])

        for k in range(SLABS + 3):
            if 2 <= k < SLABS + 2:
                deviation(k - 2)
            if k < SLABS:
                project(k)
            if 1 <= k < SLABS + 1:
                add_residual(k - 1)
            if 1 <= k <= (SEQS - 1) * HALVES:
                n, half = divmod(k + 1, HALVES)
                transpose_quarter(n, 2 * half)
                transpose_quarter(n, 2 * half + 1)
            if 2 <= k <= (SEQS - 1) * HALVES + 1:
                n, half = divmod(k, HALVES)
                quantise_half(n, half)
            if 1 <= k < SEQS:
                broadcast_mask(k)
            if k >= 3:
                normalise_and_store(k - 3)
